import numpy as np
import ml_dtypes


BF16 = ml_dtypes.bfloat16


def bf(x):
    return np.asarray(x, np.float32).astype(BF16)


def f64(x):
    return np.asarray(x).astype(np.float64)


E2M1 = np.array([0.0, 0.5, 1.0, 1.5, 2.0, 3.0, 4.0, 6.0, -0.0, -0.5, -1.0, -1.5, -2.0, -3.0, -4.0, -6.0])


def pack_weight(w, fmt):
    k, n = w.shape
    w = f64(bf(w)).reshape(k // 32, 32, n)
    amax = np.abs(w).max(1)
    if fmt == "e4m3":
        byte = np.frexp(amax)[1] - 1 + 127 - 7
    else:
        mant, ex = np.frexp(amax / 6.0)
        byte = np.where(mant > 0.5, ex, ex - 1) + 127
    byte = np.clip(np.where(amax > 0, byte, 1), 1, 254)
    scaled = (w * np.exp2(127.0 - byte)[:, None, :]).reshape(k, n).astype(np.float32)
    by_word = np.ascontiguousarray(scaled.reshape(k // 512, 128, 4, n).transpose(0, 1, 3, 2))
    if fmt == "e4m3":
        words = by_word.astype(ml_dtypes.float8_e4m3fn).view(np.uint8)
    else:
        c = by_word.astype(ml_dtypes.float4_e2m1fn).view(np.uint8) & 0xF
        words = c[..., 0::2] | (c[..., 1::2] << 4)
    return np.ascontiguousarray(words), np.ascontiguousarray(byte.astype(np.uint8).reshape(k // 512, 16, n))


def unpack_weight(words, scales, fmt):
    g, p, n, _ = words.shape
    if fmt == "e4m3":
        vals = np.ascontiguousarray(words).view(ml_dtypes.float8_e4m3fn).astype(np.float64)
    else:
        nib = np.empty((g, p, n, 4), np.uint8)
        nib[..., 0::2] = words & 0xF
        nib[..., 1::2] = words >> 4
        vals = E2M1[nib]
    vals = vals * np.repeat(np.exp2(scales.astype(np.float64) - 127.0), 8, axis=1)[..., None]
    return vals.transpose(0, 1, 3, 2).reshape(g * 512, n)

def pack4(w):
    words, scales = pack_weight(w, "e2m1")
    return words.reshape(words.shape[0], 128, -1), scales


def unpack4(words, scales):
    return unpack_weight(words.reshape(words.shape[0], 128, -1, 2), scales, "e2m1")


def kspread(k):
    return np.exp2(np.repeat(np.random.randint(-6, 7, k // 32), 32).astype(np.float64))


S, B, H, NH, HD, MAX_END = 1024, 2, 1024, 16, 64, 4096
THETA = 10000.0
HALF = HD // 2
O = NH * 2 * HD


def rope(x, cos, sin):
    xr = x.reshape(S, B, NH, HALF, 2)
    x0, x1 = xr[..., 0], xr[..., 1]
    c = cos[:, None, None, :]
    sn = sin[:, None, None, :]
    o0 = x0 * c - x1 * sn
    o1 = x0 * sn + x1 * c
    return np.stack([o0, o1], axis=-1).reshape(x.shape)


def setup_inputs():
    s = kspread(H)
    freqs = 1.0 / THETA ** (np.arange(0, HD, 2) / HD)
    ang = np.outer(np.arange(S), freqs)
    hidden_states = np.random.standard_normal((S, B, H)) * s
    hidden_states_words, hidden_states_scales = pack4(np.ascontiguousarray(hidden_states.reshape(S * B, H).T))
    w_qk = np.random.standard_normal((O, H)) / np.sqrt(H) / s
    words, scales = pack4(np.ascontiguousarray(w_qk.T))
    return {"hidden_states_words": hidden_states_words,
            "hidden_states_scales": hidden_states_scales,
            "w_qk_words": words,
            "w_qk_scales": scales,
            "cos": bf(np.cos(ang)),
            "sin": bf(np.sin(ang))}


def reference(hidden_states_words, hidden_states_scales, w_qk_words, w_qk_scales, cos, sin):
    hs = unpack4(hidden_states_words, hidden_states_scales).T.reshape(S, B, H)
    mixed = hs @ unpack4(w_qk_words, w_qk_scales)
    mixed = mixed.reshape(S, B, NH, 2 * HD)
    q, k = mixed[..., :HD], mixed[..., HD:]
    q = rope(q, f64(cos), f64(sin))
    k = rope(k, f64(cos), f64(sin))
    qb = q.transpose(1, 2, 0, 3).reshape(B * NH, S, HD)
    kb = k.transpose(1, 2, 0, 3).reshape(B * NH, S, HD)
    return qb, kb

@@ -1,0 +1,227 @@
+from contextlib import ExitStack
+
+import concourse.mybir as mybir
+
+F32 = mybir.dt.float32
+BF16 = mybir.dt.bfloat16
+I32 = mybir.dt.int32
+U8 = mybir.dt.uint8
+FP4 = mybir.dt.float4_e2m1fn_x4
+ADD = mybir.AluOpType.add
+SUB = mybir.AluOpType.subtract
+MULT = mybir.AluOpType.mult
+COPY = mybir.ActivationFunctionType.Copy
+
+P = 128
+GROUPS = 2
+TOKENS = 2048
+OUTS = 2048
+BATCH = 2
+RUN = 8
+PAIRS = 32
+HQ = 32
+BLOCKS = 8
+FLOPS = 2 * TOKENS * OUTS * 1024
+
+
+def tile_repro_pa_kernel(tc, x_words, x_scales, w_words, w_scales, cos, sin, q_rot, k_rot):
+    nc = tc.nc
+    with ExitStack() as ctx:
+        keep = ctx.enter_context(tc.tile_pool(name="keep", bufs=1))
+        xpool = ctx.enter_context(tc.tile_pool(name="xpool", bufs=4))
+        work = ctx.enter_context(tc.tile_pool(name="work", bufs=4))
+        outs = ctx.enter_context(tc.tile_pool(name="outs", bufs=2))
+        psum = ctx.enter_context(tc.psum_pool(name="psum", bufs=8))
+        ctx.enter_context(tc.manual_schedule())
+
+        x_plane = keep.tile([P, GROUPS, TOKENS], U8, align_bytes=64, name="x_plane")
+        w_plane = keep.tile([P, GROUPS, OUTS], U8, align_bytes=64, name="w_plane")
+        x_raw = keep.tile([P, GROUPS, 2 * TOKENS], U8, align_bytes=64, name="x_raw")
+        w_raw = keep.tile([P, GROUPS, 2 * OUTS], U8, align_bytes=64, name="w_raw")
+        cos_b = keep.tile([P, RUN * PAIRS], BF16, name="cos_b")
+        sin_b = keep.tile([P, RUN * PAIRS], BF16, name="sin_b")
+        c_tab = keep.tile([P, RUN * PAIRS], F32, name="c_tab")
+        s_tab = keep.tile([P, RUN * PAIRS], F32, name="s_tab")
+        n_tab = keep.tile([P, RUN * PAIRS], F32, name="n_tab")
+
+        nc.vector.memset(x_plane[:].rearrange("p g n -> p (g n)").bitcast(I32), 0)
+        nc.vector.memset(w_plane[:].rearrange("p g n -> p (g n)").bitcast(I32), 0)
+
+        def load_scales(plane, src, quarter):
+            nc.sync.dma_start(
+                out=plane[32 * quarter : 32 * quarter + 4, :, :].bitcast(I32),
+                in_=src[:, 4 * quarter : 4 * quarter + 4, :].rearrange("g r n -> r g n").bitcast(I32),
+            )
+
+        for quarter in range(4):
+            load_scales(x_plane, x_scales, quarter)
+        nc.sync.dma_start(out=w_raw[:].bitcast(I32), in_=w_words.rearrange("g p n -> p g n").bitcast(I32))
+        nc.sync.dma_start(out=x_raw[:].bitcast(I32), in_=x_words.rearrange("g p n -> p g n").bitcast(I32))
+        for quarter in range(4):
+            load_scales(w_plane, w_scales, quarter)
+        nc.gpsimd.dma_start(out=sin_b[:], in_=sin.rearrange("(p t) j -> p (t j)", t=RUN))
+        nc.gpsimd.dma_start(out=cos_b[:], in_=cos.rearrange("(p t) j -> p (t j)", t=RUN))
+
+        nc.scalar.activation(out=s_tab[:], in_=sin_b[:], func=COPY)
+        nc.scalar.activation(out=n_tab[:], in_=sin_b[:], func=COPY, scale=-1.0)
+
+        x_codes, x_scale_tiles = {}, {}
+        w_codes, w_scale_tiles = [], []
+
+        def permute_x_scales(t):
+            xs = xpool.tile([P, GROUPS, BATCH, P], U8, align_bytes=64, name="xs")
+            nc.vector.tensor_copy(
+                out=xs[:], in_=x_plane[:].rearrange("p g (q t b) -> p t g b q", t=RUN, b=BATCH)[:, t]
+            )
+            x_scale_tiles[t] = xs
+
+        def permute_x_codes(t):
+            xc = xpool.tile([P, GROUPS, BATCH, P, 2], U8, align_bytes=64, name="xc")
+            nc.vector.tensor_copy(
+                out=xc[:], in_=x_raw[:].rearrange("p g (q t b c) -> p t g b q c", t=RUN, b=BATCH, c=2)[:, t]
+            )
+            x_codes[t] = xc
+
+        def permute_w(src, bytes_per_column, block, name):
+            words = 8 * bytes_per_column // 4
+            dst = keep.tile([P, GROUPS, HQ * 4 * words], U8, align_bytes=64, name=name)
+            nc.vector.tensor_copy(
+                out=dst[:].bitcast(I32).rearrange("p g (h w) -> p g h w", w=words),
+                in_=src[:].bitcast(I32).rearrange("p g (h b w) -> p b g h w", b=BLOCKS, w=words)[:, block],
+            )
+            return dst
+
+        permute_x_scales(0)
+        nc.vector.tensor_copy(out=c_tab[:], in_=cos_b[:])
+        permute_x_scales(1)
+        for block in range(BLOCKS):
+            w_codes.append(permute_w(w_raw, 2, block, f"w_codes{block}"))
+        permute_x_codes(0)
+        for block in range(BLOCKS):
+            w_scale_tiles.append(permute_w(w_plane, 1, block, f"w_scales{block}"))
+
+        def multiply(bank, half, t, batch, block):
+            xc, xs = x_codes[t], x_scale_tiles[t]
+            for g in range(GROUPS):
+                nc.tensor.matmul_mx(
+                    out=bank[:, 256 * half : 256 * half + 256],
+                    lhsT=xc[:, g, batch].rearrange("p q c -> p (q c)").bitcast(FP4),
+                    lhsT_scale=xs[:, g, batch],
+                    rhs=w_codes[block][:, g].bitcast(FP4),
+                    rhs_scale=w_scale_tiles[block][:, g],
+                    start=(g == 0),
+                    stop=(g == GROUPS - 1),
+                )
+
+        def rotate(view, cross, turned, k, plain):
+            cs = c_tab[:, k : k + 1]
+            if plain:
+                return [
+                    lambda: nc.vector.scalar_tensor_tensor(
+                        out=turned[:, 0], in0=view[:, 0], scalar=cs, in1=cross[:, 1], op0=MULT, op1=SUB
+                    ),
+                    lambda: nc.vector.scalar_tensor_tensor(
+                        out=turned[:, 1], in0=view[:, 1], scalar=cs, in1=cross[:, 0], op0=MULT, op1=ADD
+                    ),
+                ]
+            return [
+                lambda: nc.vector.scalar_tensor_tensor(
+                    out=turned, in0=view, scalar=cs, in1=cross, op0=MULT, op1=ADD
+                )
+            ]
+
+        def cross_products(view, cross, k, plain):
+            if plain:
+                nc.scalar.activation(out=cross, in_=view, func=COPY, scale=s_tab[:, k : k + 1])
+            else:
+                nc.scalar.activation(out=cross[:, 0], in_=view[:, 1], func=COPY, scale=n_tab[:, k : k + 1])
+                nc.scalar.activation(out=cross[:, 1], in_=view[:, 0], func=COPY, scale=s_tab[:, k : k + 1])
+
+        def run_tile(t, batches, out_tile, slot, midway):
+            full = len(batches) == 2
+            columns = HQ * len(batches)
+            first = HQ * batches[0]
+            for duo in range(BLOCKS // (2 if full else 4)):
+                turned = work.tile([P, 1024], F32, name="turned")
+                rows = turned[:].rearrange("p (r c) -> p r c", c=columns)
+                for sub in range(2):
+                    bank = psum.tile([P, 512], F32, name="bank")
+                    cross = work.tile([P, 512], F32, name="cross")
+                    xrows = cross[:].rearrange("p (r c) -> p r c", c=columns)
+                    step = 2 * duo + sub
+                    if full:
+                        for half in range(2):
+                            multiply(bank, half, t, half, step)
+                        views = [bank[:].rearrange("p (c e) -> p e c", e=8)]
+                        blocks = [step]
+                    else:
+                        for half in range(2):
+                            multiply(bank, half, t, batches[0], 2 * step + half)
+                        views = [
+                            bank[:, 256 * half : 256 * half + 256].rearrange("p (c e) -> p e c", e=8)
+                            for half in range(2)
+                        ]
+                        blocks = [2 * step, 2 * step + 1]
+                    jobs = []
+                    for i, block in enumerate(blocks):
+                        for j in range(4):
+                            n = 4 * i + j
+                            plain = (not full) and j % 2 == 1
+                            view = views[i][:, 2 * j : 2 * j + 2]
+                            cr = xrows[:, 2 * n : 2 * n + 2]
+                            base = 8 * len(blocks) * sub
+                            tr = rows[:, base + 2 * n : base + 2 * n + 2]
+                            k = PAIRS * t + 4 * block + j
+                            cross_products(view, cr, k, plain)
+                            jobs.extend(rotate(view, cr, tr, k, plain))
+                    for job in jobs:
+                        job()
+                width = 2 * 512 // columns
+                nc.gpsimd.tensor_scalar(
+                    out=out_tile[:, first : first + columns, slot, width * duo : width * duo + width].rearrange(
+                        "p c (j r) -> p j c r", r=4
+                    ),
+                    in0=rows.rearrange("p (j r) c -> p j c r", r=4),
+                    scalar1=1.0,
+                    scalar2=0.0,
+                    op0=MULT,
+                    op1=ADD,
+                )
+                if 2 * duo + 2 == BLOCKS // (2 if full else 4):
+                    midway()
+
+        def store(out_tile, batch, t0):
+            heads = out_tile[:, HQ * batch : HQ * batch + HQ].rearrange("p (h s) t d -> p s h (t d)", s=2)
+            for s, dst in enumerate((q_rot, k_rot)):
+                nc.sync.dma_start(
+                    out=dst[16 * batch : 16 * batch + 16]
+                    .rearrange("h (p t) d -> p h t d", t=RUN)[:, :, t0 : t0 + 2]
+                    .rearrange("p h t d -> p h (t d)"),
+                    in_=heads[:, s],
+                )
+
+        def nothing():
+            return None
+
+        def prepare(t):
+            def run():
+                permute_x_scales(t)
+                permute_x_codes(t)
+
+            return run
+
+        permute_x_codes(1)
+        for t0 in range(0, RUN, 2):
+            out_tile = outs.tile([P, BATCH * HQ, 2, 64], F32, name="out_tile")
+            nxt = prepare(t0 + 2) if t0 + 2 < RUN else nothing
+            nxt2 = prepare(t0 + 3) if t0 + 3 < RUN else nothing
+            if t0 in (0, RUN - 2):
+                for batch in range(BATCH):
+                    run_tile(t0, (batch,), out_tile, 0, nothing if batch == 0 else nxt2)
+                    run_tile(t0 + 1, (batch,), out_tile, 1, nxt if batch == 0 else nothing)
+                    store(out_tile, batch, t0)
+            else:
+                run_tile(t0, (0, 1), out_tile, 0, nxt)
+                run_tile(t0 + 1, (0, 1), out_tile, 1, nxt2)
+                for batch in range(BATCH):
+                    store(out_tile, batch, t0)

@@ -20,7 +20,9 @@ BATCH = 2
 RUN = 8
 PAIRS = 32
 HQ = 32
+COLUMNS = BATCH * HQ
 BLOCKS = 8
+PLAIN = ()
 FLOPS = 2 * TOKENS * OUTS * 1024
 
 
@@ -44,26 +46,26 @@ def tile_repro_pa_kernel(tc, x_words, x_scales, w_words, w_scales, cos, sin, q_r
         s_tab = keep.tile([P, RUN * PAIRS], F32, name="s_tab")
         n_tab = keep.tile([P, RUN * PAIRS], F32, name="n_tab")
 
-        nc.vector.memset(x_plane[:].rearrange("p g n -> p (g n)").bitcast(I32), 0)
-        nc.vector.memset(w_plane[:].rearrange("p g n -> p (g n)").bitcast(I32), 0)
-
         def load_scales(plane, src, quarter):
             nc.sync.dma_start(
                 out=plane[32 * quarter : 32 * quarter + 4, :, :].bitcast(I32),
                 in_=src[:, 4 * quarter : 4 * quarter + 4, :].rearrange("g r n -> r g n").bitcast(I32),
             )
 
-        for quarter in range(4):
-            load_scales(x_plane, x_scales, quarter)
-        nc.sync.dma_start(out=w_raw[:].bitcast(I32), in_=w_words.rearrange("g p n -> p g n").bitcast(I32))
-        nc.sync.dma_start(out=x_raw[:].bitcast(I32), in_=x_words.rearrange("g p n -> p g n").bitcast(I32))
-        for quarter in range(4):
-            load_scales(w_plane, w_scales, quarter)
+        nc.vector.memset(x_plane[:].rearrange("p g n -> p (g n)").bitcast(I32), 0)
         nc.gpsimd.dma_start(out=sin_b[:], in_=sin.rearrange("(p t) j -> p (t j)", t=RUN))
         nc.gpsimd.dma_start(out=cos_b[:], in_=cos.rearrange("(p t) j -> p (t j)", t=RUN))
+        nc.vector.memset(w_plane[:].rearrange("p g n -> p (g n)").bitcast(I32), 0)
+        for quarter in range(4):
+            load_scales(x_plane, x_scales, quarter)
+        nc.sync.dma_start(out=x_raw[:].bitcast(I32), in_=x_words.rearrange("g p n -> p g n").bitcast(I32))
+        nc.sync.dma_start(out=w_raw[:].bitcast(I32), in_=w_words.rearrange("g p n -> p g n").bitcast(I32))
+        for quarter in range(4):
+            load_scales(w_plane, w_scales, quarter)
 
         nc.scalar.activation(out=s_tab[:], in_=sin_b[:], func=COPY)
         nc.scalar.activation(out=n_tab[:], in_=sin_b[:], func=COPY, scale=-1.0)
+        nc.scalar.activation(out=c_tab[:], in_=cos_b[:], func=COPY)
 
         x_codes, x_scale_tiles = {}, {}
         w_codes, w_scale_tiles = [], []
@@ -92,19 +94,18 @@ def tile_repro_pa_kernel(tc, x_words, x_scales, w_words, w_scales, cos, sin, q_r
             return dst
 
         permute_x_scales(0)
-        nc.vector.tensor_copy(out=c_tab[:], in_=cos_b[:])
         permute_x_scales(1)
-        for block in range(BLOCKS):
-            w_codes.append(permute_w(w_raw, 2, block, f"w_codes{block}"))
         permute_x_codes(0)
         for block in range(BLOCKS):
+            w_codes.append(permute_w(w_raw, 2, block, f"w_codes{block}"))
             w_scale_tiles.append(permute_w(w_plane, 1, block, f"w_scales{block}"))
+        permute_x_codes(1)
 
-        def multiply(bank, half, t, batch, block):
+        def multiply(bank, t, batch, block):
             xc, xs = x_codes[t], x_scale_tiles[t]
             for g in range(GROUPS):
                 nc.tensor.matmul_mx(
-                    out=bank[:, 256 * half : 256 * half + 256],
+                    out=bank[:, 256 * batch : 256 * batch + 256],
                     lhsT=xc[:, g, batch].rearrange("p q c -> p (q c)").bitcast(FP4),
                     lhsT_scale=xs[:, g, batch],
                     rhs=w_codes[block][:, g].bitcast(FP4),
@@ -113,23 +114,6 @@ def tile_repro_pa_kernel(tc, x_words, x_scales, w_words, w_scales, cos, sin, q_r
                     stop=(g == GROUPS - 1),
                 )
 
-        def rotate(view, cross, turned, k, plain):
-            cs = c_tab[:, k : k + 1]
-            if plain:
-                return [
-                    lambda: nc.vector.scalar_tensor_tensor(
-                        out=turned[:, 0], in0=view[:, 0], scalar=cs, in1=cross[:, 1], op0=MULT, op1=SUB
-                    ),
-                    lambda: nc.vector.scalar_tensor_tensor(
-                        out=turned[:, 1], in0=view[:, 1], scalar=cs, in1=cross[:, 0], op0=MULT, op1=ADD
-                    ),
-                ]
-            return [
-                lambda: nc.vector.scalar_tensor_tensor(
-                    out=turned, in0=view, scalar=cs, in1=cross, op0=MULT, op1=ADD
-                )
-            ]
-
         def cross_products(view, cross, k, plain):
             if plain:
                 nc.scalar.activation(out=cross, in_=view, func=COPY, scale=s_tab[:, k : k + 1])
@@ -137,58 +121,44 @@ def tile_repro_pa_kernel(tc, x_words, x_scales, w_words, w_scales, cos, sin, q_r
                 nc.scalar.activation(out=cross[:, 0], in_=view[:, 1], func=COPY, scale=n_tab[:, k : k + 1])
                 nc.scalar.activation(out=cross[:, 1], in_=view[:, 0], func=COPY, scale=s_tab[:, k : k + 1])
 
-        def run_tile(t, batches, out_tile, slot, midway):
-            full = len(batches) == 2
-            columns = HQ * len(batches)
-            first = HQ * batches[0]
-            for duo in range(BLOCKS // (2 if full else 4)):
-                turned = work.tile([P, 1024], F32, name="turned")
-                rows = turned[:].rearrange("p (r c) -> p r c", c=columns)
+        def rotate(view, cross, turned, k, plain):
+            cs = c_tab[:, k : k + 1]
+            if plain:
+                nc.vector.scalar_tensor_tensor(
+                    out=turned[:, 0], in0=view[:, 0], scalar=cs, in1=cross[:, 1], op0=MULT, op1=SUB
+                )
+                nc.vector.scalar_tensor_tensor(
+                    out=turned[:, 1], in0=view[:, 1], scalar=cs, in1=cross[:, 0], op0=MULT, op1=ADD
+                )
+            else:
+                nc.vector.scalar_tensor_tensor(out=turned, in0=view, scalar=cs, in1=cross, op0=MULT, op1=ADD)
+
+        def run_tile(t, out_tile, slot):
+            for duo in range(BLOCKS // 2):
+                turned = work.tile([P, 16, COLUMNS], F32, name="turned")
                 for sub in range(2):
+                    block = 2 * duo + sub
                     bank = psum.tile([P, 512], F32, name="bank")
-                    cross = work.tile([P, 512], F32, name="cross")
-                    xrows = cross[:].rearrange("p (r c) -> p r c", c=columns)
-                    step = 2 * duo + sub
-                    if full:
-                        for half in range(2):
-                            multiply(bank, half, t, half, step)
-                        views = [bank[:].rearrange("p (c e) -> p e c", e=8)]
-                        blocks = [step]
-                    else:
-                        for half in range(2):
-                            multiply(bank, half, t, batches[0], 2 * step + half)
-                        views = [
-                            bank[:, 256 * half : 256 * half + 256].rearrange("p (c e) -> p e c", e=8)
-                            for half in range(2)
-                        ]
-                        blocks = [2 * step, 2 * step + 1]
-                    jobs = []
-                    for i, block in enumerate(blocks):
-                        for j in range(4):
-                            n = 4 * i + j
-                            plain = (not full) and j % 2 == 1
-                            view = views[i][:, 2 * j : 2 * j + 2]
-                            cr = xrows[:, 2 * n : 2 * n + 2]
-                            base = 8 * len(blocks) * sub
-                            tr = rows[:, base + 2 * n : base + 2 * n + 2]
-                            k = PAIRS * t + 4 * block + j
-                            cross_products(view, cr, k, plain)
-                            jobs.extend(rotate(view, cr, tr, k, plain))
-                    for job in jobs:
-                        job()
-                width = 2 * 512 // columns
+                    cross = work.tile([P, 8, COLUMNS], F32, name="cross")
+                    for batch in range(BATCH):
+                        multiply(bank, t, batch, block)
+                    view = bank[:].rearrange("p (c e) -> p e c", e=8)
+                    for j in range(4):
+                        cross_products(view[:, 2 * j : 2 * j + 2], cross[:, 2 * j : 2 * j + 2], PAIRS * t + 4 * block + j, j in PLAIN)
+                    for j in reversed(range(4)):
+                        r = 8 * sub + 2 * j
+                        rotate(view[:, 2 * j : 2 * j + 2], cross[:, 2 * j : 2 * j + 2], turned[:, r : r + 2], PAIRS * t + 4 * block + j, j in PLAIN)
                 nc.gpsimd.tensor_scalar(
-                    out=out_tile[:, first : first + columns, slot, width * duo : width * duo + width].rearrange(
-                        "p c (j r) -> p j c r", r=4
-                    ),
-                    in0=rows.rearrange("p (j r) c -> p j c r", r=4),
+                    out=out_tile[:, :, slot, 16 * duo : 16 * duo + 16].rearrange("p c (j r) -> p j c r", r=4),
+                    in0=turned[:].rearrange("p (j r) c -> p j c r", r=4),
                     scalar1=1.0,
                     scalar2=0.0,
                     op0=MULT,
                     op1=ADD,
                 )
-                if 2 * duo + 2 == BLOCKS // (2 if full else 4):
-                    midway()
+                if duo == 1 and t + 2 < RUN:
+                    permute_x_scales(t + 2)
+                    permute_x_codes(t + 2)
 
         def store(out_tile, batch, t0):
             heads = out_tile[:, HQ * batch : HQ * batch + HQ].rearrange("p (h s) t d -> p s h (t d)", s=2)
@@ -200,28 +170,9 @@ def tile_repro_pa_kernel(tc, x_words, x_scales, w_words, w_scales, cos, sin, q_r
                     in_=heads[:, s],
                 )
 
-        def nothing():
-            return None
-
-        def prepare(t):
-            def run():
-                permute_x_scales(t)
-                permute_x_codes(t)
-
-            return run
-
-        permute_x_codes(1)
         for t0 in range(0, RUN, 2):
-            out_tile = outs.tile([P, BATCH * HQ, 2, 64], F32, name="out_tile")
-            nxt = prepare(t0 + 2) if t0 + 2 < RUN else nothing
-            nxt2 = prepare(t0 + 3) if t0 + 3 < RUN else nothing
-            if t0 in (0, RUN - 2):
-                for batch in range(BATCH):
-                    run_tile(t0, (batch,), out_tile, 0, nothing if batch == 0 else nxt2)
-                    run_tile(t0 + 1, (batch,), out_tile, 1, nxt if batch == 0 else nothing)
-                    store(out_tile, batch, t0)
-            else:
-                run_tile(t0, (0, 1), out_tile, 0, nxt)
-                run_tile(t0 + 1, (0, 1), out_tile, 1, nxt2)
-                for batch in range(BATCH):
-                    store(out_tile, batch, t0)
+            out_tile = outs.tile([P, COLUMNS, 2, 64], F32, name="out_tile")
+            run_tile(t0, out_tile, 0)
+            run_tile(t0 + 1, out_tile, 1)
+            for batch in range(BATCH):
+                store(out_tile, batch, t0)

@@ -30,7 +30,7 @@ def tile_repro_pa_kernel(tc, x_words, x_scales, w_words, w_scales, cos, sin, q_r
     nc = tc.nc
     with ExitStack() as ctx:
         keep = ctx.enter_context(tc.tile_pool(name="keep", bufs=1))
-        xpool = ctx.enter_context(tc.tile_pool(name="xpool", bufs=4))
+        xpool = ctx.enter_context(tc.tile_pool(name="xpool", bufs=RUN))
         work = ctx.enter_context(tc.tile_pool(name="work", bufs=4))
         outs = ctx.enter_context(tc.tile_pool(name="outs", bufs=2))
         psum = ctx.enter_context(tc.psum_pool(name="psum", bufs=8))
@@ -93,13 +93,14 @@ def tile_repro_pa_kernel(tc, x_words, x_scales, w_words, w_scales, cos, sin, q_r
             )
             return dst
 
-        permute_x_scales(0)
-        permute_x_scales(1)
+        for t in range(RUN):
+            permute_x_scales(t)
         permute_x_codes(0)
         for block in range(BLOCKS):
             w_codes.append(permute_w(w_raw, 2, block, f"w_codes{block}"))
             w_scale_tiles.append(permute_w(w_plane, 1, block, f"w_scales{block}"))
-        permute_x_codes(1)
+        for t in range(1, RUN):
+            permute_x_codes(t)
 
         def multiply(bank, t, batch, block):
             xc, xs = x_codes[t], x_scale_tiles[t]
@@ -156,23 +157,21 @@ def tile_repro_pa_kernel(tc, x_words, x_scales, w_words, w_scales, cos, sin, q_r
                     op0=MULT,
                     op1=ADD,
                 )
-                if duo == 1 and t + 2 < RUN:
-                    permute_x_scales(t + 2)
-                    permute_x_codes(t + 2)
 
-        def store(out_tile, batch, t0):
-            heads = out_tile[:, HQ * batch : HQ * batch + HQ].rearrange("p (h s) t d -> p s h (t d)", s=2)
+        def store(out_tile, batch, t0, slots):
+            heads = out_tile[:, HQ * batch : HQ * batch + HQ, slots].rearrange("p (h s) t d -> p s h t d", s=2)
+            first, last = t0 + slots.start, t0 + slots.stop
             for s, dst in enumerate((q_rot, k_rot)):
                 nc.sync.dma_start(
                     out=dst[16 * batch : 16 * batch + 16]
-                    .rearrange("h (p t) d -> p h t d", t=RUN)[:, :, t0 : t0 + 2]
+                    .rearrange("h (p t) d -> p h t d", t=RUN)[:, :, first:last]
                     .rearrange("p h t d -> p h (t d)"),
-                    in_=heads[:, s],
+                    in_=heads[:, s].rearrange("p h t d -> p h (t d)"),
                 )
 
         for t0 in range(0, RUN, 2):
             out_tile = outs.tile([P, COLUMNS, 2, 64], F32, name="out_tile")
-            run_tile(t0, out_tile, 0)
-            run_tile(t0 + 1, out_tile, 1)
+            for slot in range(2):
+                run_tile(t0 + slot, out_tile, slot)
             for batch in range(BATCH):
-                store(out_tile, batch, t0)
+                store(out_tile, batch, t0, slice(0, 2))

@@ -102,11 +102,11 @@ def tile_repro_pa_kernel(tc, x_words, x_scales, w_words, w_scales, cos, sin, q_r
         for t in range(1, RUN):
             permute_x_codes(t)
 
-        def multiply(bank, t, batch, block):
+        def multiply(out, t, batch, block):
             xc, xs = x_codes[t], x_scale_tiles[t]
             for g in range(GROUPS):
                 nc.tensor.matmul_mx(
-                    out=bank[:, 256 * batch : 256 * batch + 256],
+                    out=out,
                     lhsT=xc[:, g, batch].rearrange("p q c -> p (q c)").bitcast(FP4),
                     lhsT_scale=xs[:, g, batch],
                     rhs=w_codes[block][:, g].bitcast(FP4),
@@ -115,43 +115,54 @@ def tile_repro_pa_kernel(tc, x_words, x_scales, w_words, w_scales, cos, sin, q_r
                     stop=(g == GROUPS - 1),
                 )
 
-        def cross_products(view, cross, k, plain):
-            if plain:
-                nc.scalar.activation(out=cross, in_=view, func=COPY, scale=s_tab[:, k : k + 1])
-            else:
-                nc.scalar.activation(out=cross[:, 0], in_=view[:, 1], func=COPY, scale=n_tab[:, k : k + 1])
-                nc.scalar.activation(out=cross[:, 1], in_=view[:, 0], func=COPY, scale=s_tab[:, k : k + 1])
-
-        def rotate(view, cross, turned, k, plain):
-            cs = c_tab[:, k : k + 1]
-            if plain:
-                nc.vector.scalar_tensor_tensor(
-                    out=turned[:, 0], in0=view[:, 0], scalar=cs, in1=cross[:, 1], op0=MULT, op1=SUB
-                )
-                nc.vector.scalar_tensor_tensor(
-                    out=turned[:, 1], in0=view[:, 1], scalar=cs, in1=cross[:, 0], op0=MULT, op1=ADD
-                )
-            else:
-                nc.vector.scalar_tensor_tensor(out=turned, in0=view, scalar=cs, in1=cross, op0=MULT, op1=ADD)
-
-        def run_tile(t, out_tile, slot):
-            for duo in range(BLOCKS // 2):
-                turned = work.tile([P, 16, COLUMNS], F32, name="turned")
+        def run_tile(t, batches, out_tile, slot):
+            columns = HQ * len(batches)
+            first = HQ * batches[0]
+            duos = BLOCKS * len(batches) // 4
+            width = 2048 // columns // 2
+            for duo in range(duos):
+                turned = work.tile([P, 1024], F32, name="turned")
+                rows = turned[:].rearrange("p (i j c r) -> p i j c r", i=2, c=columns, r=2)
                 for sub in range(2):
-                    block = 2 * duo + sub
                     bank = psum.tile([P, 512], F32, name="bank")
-                    cross = work.tile([P, 8, COLUMNS], F32, name="cross")
-                    for batch in range(BATCH):
-                        multiply(bank, t, batch, block)
-                    view = bank[:].rearrange("p (c e) -> p e c", e=8)
-                    for j in range(4):
-                        cross_products(view[:, 2 * j : 2 * j + 2], cross[:, 2 * j : 2 * j + 2], PAIRS * t + 4 * block + j, j in PLAIN)
-                    for j in reversed(range(4)):
-                        r = 8 * sub + 2 * j
-                        rotate(view[:, 2 * j : 2 * j + 2], cross[:, 2 * j : 2 * j + 2], turned[:, r : r + 2], PAIRS * t + 4 * block + j, j in PLAIN)
+                    cross = work.tile([P, 512], F32, name="cross")
+                    crows = cross[:].rearrange("p (n r c) -> p n r c", r=2, c=columns)
+                    jobs = []
+                    for half in range(2):
+                        if len(batches) == 2:
+                            batch, block = half, 2 * duo + sub
+                        else:
+                            batch, block = batches[0], 4 * duo + 2 * sub + half
+                        multiply(bank[:, 256 * half : 256 * half + 256], t, batch, block)
+                    if len(batches) == 2:
+                        views = [(2 * duo + sub, bank[:].rearrange("p (c e) -> p c e", e=8))]
+                    else:
+                        views = [
+                            (4 * duo + 2 * sub + half, bank[:, 256 * half : 256 * half + 256].rearrange("p (c e) -> p c e", e=8))
+                            for half in range(2)
+                        ]
+                    for i, (block, view) in enumerate(views):
+                        for j in range(4):
+                            n = 4 * i + j
+                            k = PAIRS * t + 4 * block + j
+                            nc.scalar.activation(out=crows[:, n, 0], in_=view[:, :, 2 * j + 1], func=COPY, scale=n_tab[:, k : k + 1])
+                            nc.scalar.activation(out=crows[:, n, 1], in_=view[:, :, 2 * j], func=COPY, scale=s_tab[:, k : k + 1])
+                            jobs.append((n, k, view[:, :, 2 * j : 2 * j + 2]))
+                    for n, k, pair in reversed(jobs):
+                        pos = len(jobs) * sub + n
+                        nc.vector.scalar_tensor_tensor(
+                            out=rows[:, pos % 2, pos // 2],
+                            in0=pair,
+                            scalar=c_tab[:, k : k + 1],
+                            in1=crows[:, n].rearrange("p r c -> p c r"),
+                            op0=MULT,
+                            op1=ADD,
+                        )
                 nc.gpsimd.tensor_scalar(
-                    out=out_tile[:, :, slot, 16 * duo : 16 * duo + 16].rearrange("p c (j r) -> p j c r", r=4),
-                    in0=turned[:].rearrange("p (j r) c -> p j c r", r=4),
+                    out=out_tile[:, first : first + columns, slot, width * duo : width * duo + width].rearrange(
+                        "p c (j i r) -> p j c i r", i=2, r=2
+                    ),
+                    in0=rows.rearrange("p i j c r -> p j c i r"),
                     scalar1=1.0,
                     scalar2=0.0,
                     op0=MULT,
@@ -171,7 +182,8 @@ def tile_repro_pa_kernel(tc, x_words, x_scales, w_words, w_scales, cos, sin, q_r
 
         for t0 in range(0, RUN, 2):
             out_tile = outs.tile([P, COLUMNS, 2, 64], F32, name="out_tile")
-            for slot in range(2):
-                run_tile(t0 + slot, out_tile, slot)
-            for batch in range(BATCH):
-                store(out_tile, batch, t0, slice(0, 2))
+            for batches in ((0, 1),) if t0 < 8 else ((0,), (1,)):
+                for slot in range(2):
+                    run_tile(t0 + slot, batches, out_tile, slot)
+                for batch in batches:
+                    store(out_tile, batch, t0, slice(0, 2))

@@ -8,7 +8,6 @@ I32 = mybir.dt.int32
 U8 = mybir.dt.uint8
 FP4 = mybir.dt.float4_e2m1fn_x4
 ADD = mybir.AluOpType.add
-SUB = mybir.AluOpType.subtract
 MULT = mybir.AluOpType.mult
 COPY = mybir.ActivationFunctionType.Copy
 
@@ -17,12 +16,13 @@ GROUPS = 2
 TOKENS = 2048
 OUTS = 2048
 BATCH = 2
-RUN = 8
+TILES = 8
 PAIRS = 32
-HQ = 32
-COLUMNS = BATCH * HQ
+DIM = 2 * PAIRS
+HS = 32
 BLOCKS = 8
-PLAIN = ()
+BLOCK = 256
+BANK = 512
 FLOPS = 2 * TOKENS * OUTS * 1024
 
 
@@ -30,9 +30,9 @@ def tile_repro_pa_kernel(tc, x_words, x_scales, w_words, w_scales, cos, sin, q_r
     nc = tc.nc
     with ExitStack() as ctx:
         keep = ctx.enter_context(tc.tile_pool(name="keep", bufs=1))
-        xpool = ctx.enter_context(tc.tile_pool(name="xpool", bufs=RUN))
         work = ctx.enter_context(tc.tile_pool(name="work", bufs=4))
-        outs = ctx.enter_context(tc.tile_pool(name="outs", bufs=2))
+        sines = ctx.enter_context(tc.tile_pool(name="sines", bufs=6))
+        outs = ctx.enter_context(tc.tile_pool(name="outs", bufs=3))
         psum = ctx.enter_context(tc.psum_pool(name="psum", bufs=8))
         ctx.enter_context(tc.manual_schedule())
 
@@ -40,150 +40,177 @@ def tile_repro_pa_kernel(tc, x_words, x_scales, w_words, w_scales, cos, sin, q_r
         w_plane = keep.tile([P, GROUPS, OUTS], U8, align_bytes=64, name="w_plane")
         x_raw = keep.tile([P, GROUPS, 2 * TOKENS], U8, align_bytes=64, name="x_raw")
         w_raw = keep.tile([P, GROUPS, 2 * OUTS], U8, align_bytes=64, name="w_raw")
-        cos_b = keep.tile([P, RUN * PAIRS], BF16, name="cos_b")
-        sin_b = keep.tile([P, RUN * PAIRS], BF16, name="sin_b")
-        c_tab = keep.tile([P, RUN * PAIRS], F32, name="c_tab")
-        s_tab = keep.tile([P, RUN * PAIRS], F32, name="s_tab")
-        n_tab = keep.tile([P, RUN * PAIRS], F32, name="n_tab")
+        cos_in = keep.tile([P, TILES * PAIRS], BF16, name="cos_in")
+        sin_in = keep.tile([P, TILES * PAIRS], BF16, name="sin_in")
+        cos_tab = keep.tile([P, TILES * PAIRS], F32, name="cos_tab")
+        sin_tab = keep.tile([P, TILES * PAIRS], F32, name="sin_tab")
+        neg_tab = keep.tile([P, TILES * PAIRS], F32, name="neg_tab")
 
-        def load_scales(plane, src, quarter):
-            nc.sync.dma_start(
-                out=plane[32 * quarter : 32 * quarter + 4, :, :].bitcast(I32),
-                in_=src[:, 4 * quarter : 4 * quarter + 4, :].rearrange("g r n -> r g n").bitcast(I32),
-            )
+        def load_codes(tile, words):
+            nc.sync.dma_start(out=tile[:].bitcast(I32), in_=words.rearrange("g p n -> p g n").bitcast(I32))
+
+        def load_scales(plane, scales):
+            for quad in range(4):
+                nc.sync.dma_start(
+                    out=plane[32 * quad : 32 * quad + 4].bitcast(I32),
+                    in_=scales[:, 4 * quad : 4 * quad + 4].rearrange("g r n -> r g n").bitcast(I32),
+                )
 
         nc.vector.memset(x_plane[:].rearrange("p g n -> p (g n)").bitcast(I32), 0)
-        nc.gpsimd.dma_start(out=sin_b[:], in_=sin.rearrange("(p t) j -> p (t j)", t=RUN))
-        nc.gpsimd.dma_start(out=cos_b[:], in_=cos.rearrange("(p t) j -> p (t j)", t=RUN))
         nc.vector.memset(w_plane[:].rearrange("p g n -> p (g n)").bitcast(I32), 0)
-        for quarter in range(4):
-            load_scales(x_plane, x_scales, quarter)
-        nc.sync.dma_start(out=x_raw[:].bitcast(I32), in_=x_words.rearrange("g p n -> p g n").bitcast(I32))
-        nc.sync.dma_start(out=w_raw[:].bitcast(I32), in_=w_words.rearrange("g p n -> p g n").bitcast(I32))
-        for quarter in range(4):
-            load_scales(w_plane, w_scales, quarter)
+        load_scales(x_plane, x_scales)
+        load_codes(x_raw, x_words)
+        load_codes(w_raw, w_words)
+        load_scales(w_plane, w_scales)
+        nc.gpsimd.dma_start(out=sin_in[:], in_=sin.rearrange("(p t) j -> p (t j)", t=TILES))
+        nc.gpsimd.dma_start(out=cos_in[:], in_=cos.rearrange("(p t) j -> p (t j)", t=TILES))
+        nc.scalar.activation(out=sin_tab[:], in_=sin_in[:], func=COPY)
+        nc.scalar.activation(out=neg_tab[:], in_=sin_in[:], func=COPY, scale=-1.0)
+        nc.scalar.activation(out=cos_tab[:], in_=cos_in[:], func=COPY)
 
-        nc.scalar.activation(out=s_tab[:], in_=sin_b[:], func=COPY)
-        nc.scalar.activation(out=n_tab[:], in_=sin_b[:], func=COPY, scale=-1.0)
-        nc.scalar.activation(out=c_tab[:], in_=cos_b[:], func=COPY)
+        x_codes, x_bytes, w_codes, w_bytes = [], [], [], []
 
-        x_codes, x_scale_tiles = {}, {}
-        w_codes, w_scale_tiles = [], []
-
-        def permute_x_scales(t):
-            xs = xpool.tile([P, GROUPS, BATCH, P], U8, align_bytes=64, name="xs")
+        def order_x_bytes(t):
+            tile = keep.tile([P, GROUPS, BATCH, P], U8, align_bytes=64, name=f"x_bytes{t}")
             nc.vector.tensor_copy(
-                out=xs[:], in_=x_plane[:].rearrange("p g (q t b) -> p t g b q", t=RUN, b=BATCH)[:, t]
+                out=tile[:], in_=x_plane[:].rearrange("p g (q t b) -> p t g b q", t=TILES, b=BATCH)[:, t]
             )
-            x_scale_tiles[t] = xs
+            x_bytes.append(tile)
 
-        def permute_x_codes(t):
-            xc = xpool.tile([P, GROUPS, BATCH, P, 2], U8, align_bytes=64, name="xc")
+        def order_x_codes(t):
+            tile = keep.tile([P, GROUPS, BATCH, P, 2], U8, align_bytes=64, name=f"x_codes{t}")
             nc.vector.tensor_copy(
-                out=xc[:], in_=x_raw[:].rearrange("p g (q t b c) -> p t g b q c", t=RUN, b=BATCH, c=2)[:, t]
+                out=tile[:], in_=x_raw[:].rearrange("p g (q t b c) -> p t g b q c", t=TILES, b=BATCH, c=2)[:, t]
             )
-            x_codes[t] = xc
+            x_codes.append(tile)
 
-        def permute_w(src, bytes_per_column, block, name):
-            words = 8 * bytes_per_column // 4
-            dst = keep.tile([P, GROUPS, HQ * 4 * words], U8, align_bytes=64, name=name)
+        def order_w(source, width, name, block):
+            words = 8 * width // 4
+            tile = keep.tile([P, GROUPS, BLOCK * width], U8, align_bytes=64, name=f"{name}{block}")
             nc.vector.tensor_copy(
-                out=dst[:].bitcast(I32).rearrange("p g (h w) -> p g h w", w=words),
-                in_=src[:].bitcast(I32).rearrange("p g (h b w) -> p b g h w", b=BLOCKS, w=words)[:, block],
+                out=tile[:].bitcast(I32).rearrange("p g (h w) -> p g h w", w=words),
+                in_=source[:].bitcast(I32).rearrange("p g (h i w) -> p i g h w", i=BLOCKS, w=words)[:, block],
             )
-            return dst
+            return tile
 
-        for t in range(RUN):
-            permute_x_scales(t)
-        permute_x_codes(0)
+        for t in range(TILES):
+            order_x_bytes(t)
+        order_x_codes(0)
         for block in range(BLOCKS):
-            w_codes.append(permute_w(w_raw, 2, block, f"w_codes{block}"))
-            w_scale_tiles.append(permute_w(w_plane, 1, block, f"w_scales{block}"))
-        for t in range(1, RUN):
-            permute_x_codes(t)
+            w_codes.append(order_w(w_raw, 2, "w_codes", block))
+            w_bytes.append(order_w(w_plane, 1, "w_bytes", block))
 
-        def multiply(out, t, batch, block):
-            xc, xs = x_codes[t], x_scale_tiles[t]
+        def multiply(out, t, batch, codes, scales):
             for g in range(GROUPS):
                 nc.tensor.matmul_mx(
                     out=out,
-                    lhsT=xc[:, g, batch].rearrange("p q c -> p (q c)").bitcast(FP4),
-                    lhsT_scale=xs[:, g, batch],
-                    rhs=w_codes[block][:, g].bitcast(FP4),
-                    rhs_scale=w_scale_tiles[block][:, g],
+                    lhsT=x_codes[t][:, g, batch].rearrange("p q c -> p (q c)").bitcast(FP4),
+                    lhsT_scale=x_bytes[t][:, g, batch],
+                    rhs=codes[:, g].bitcast(FP4),
+                    rhs_scale=scales[:, g],
                     start=(g == 0),
                     stop=(g == GROUPS - 1),
                 )
 
-        def run_tile(t, batches, out_tile, slot):
-            columns = HQ * len(batches)
-            first = HQ * batches[0]
-            duos = BLOCKS * len(batches) // 4
-            width = 2048 // columns // 2
-            for duo in range(duos):
-                turned = work.tile([P, 1024], F32, name="turned")
-                rows = turned[:].rearrange("p (i j c r) -> p i j c r", i=2, c=columns, r=2)
+        def rotate_pairs(t, columns, jobs, turned):
+            product = sines.tile([P, BANK], F32, name="product")
+            rows = product[:].rearrange("p (n r c) -> p n r c", r=2, c=columns)
+            for n, (k, x) in enumerate(jobs):
+                at = slice(PAIRS * t + k, PAIRS * t + k + 1)
+                nc.scalar.activation(out=rows[:, n, 0], in_=x[:, :, 1], func=COPY, scale=neg_tab[:, at])
+                nc.scalar.activation(out=rows[:, n, 1], in_=x[:, :, 0], func=COPY, scale=sin_tab[:, at])
+            for n, (k, x) in reversed(list(enumerate(jobs))):
+                nc.vector.scalar_tensor_tensor(
+                    out=turned(n),
+                    in0=x,
+                    scalar=cos_tab[:, PAIRS * t + k : PAIRS * t + k + 1],
+                    in1=rows[:, n].rearrange("p r c -> p c r"),
+                    op0=MULT,
+                    op1=ADD,
+                )
+
+        def narrow(t, batches, result):
+            columns = HS * len(batches)
+            per_bank = 2 // len(batches)
+            for first in range(0, BLOCKS, 2 * per_bank):
+                turned = work.tile([P, 2 * BANK], F32, name="turned")
+                grid = turned[:].rearrange("p (i m c r) -> p i m c r", i=2, c=columns, r=2)
                 for sub in range(2):
-                    bank = psum.tile([P, 512], F32, name="bank")
-                    cross = work.tile([P, 512], F32, name="cross")
-                    crows = cross[:].rearrange("p (n r c) -> p n r c", r=2, c=columns)
+                    start = first + sub * per_bank
+                    bank = psum.tile([P, BANK], F32, name="bank")
+                    halves = [(b, start + i) for i in range(per_bank) for b in batches]
+                    for half, (b, block) in enumerate(halves):
+                        multiply(bank[:, BLOCK * half : BLOCK * half + BLOCK], t, b, w_codes[block], w_bytes[block])
                     jobs = []
-                    for half in range(2):
-                        if len(batches) == 2:
-                            batch, block = half, 2 * duo + sub
-                        else:
-                            batch, block = batches[0], 4 * duo + 2 * sub + half
-                        multiply(bank[:, 256 * half : 256 * half + 256], t, batch, block)
-                    if len(batches) == 2:
-                        views = [(2 * duo + sub, bank[:].rearrange("p (c e) -> p c e", e=8))]
-                    else:
-                        views = [
-                            (4 * duo + 2 * sub + half, bank[:, 256 * half : 256 * half + 256].rearrange("p (c e) -> p c e", e=8))
-                            for half in range(2)
-                        ]
-                    for i, (block, view) in enumerate(views):
-                        for j in range(4):
-                            n = 4 * i + j
-                            k = PAIRS * t + 4 * block + j
-                            nc.scalar.activation(out=crows[:, n, 0], in_=view[:, :, 2 * j + 1], func=COPY, scale=n_tab[:, k : k + 1])
-                            nc.scalar.activation(out=crows[:, n, 1], in_=view[:, :, 2 * j], func=COPY, scale=s_tab[:, k : k + 1])
-                            jobs.append((n, k, view[:, :, 2 * j : 2 * j + 2]))
-                    for n, k, pair in reversed(jobs):
-                        pos = len(jobs) * sub + n
-                        nc.vector.scalar_tensor_tensor(
-                            out=rows[:, pos % 2, pos // 2],
-                            in0=pair,
-                            scalar=c_tab[:, k : k + 1],
-                            in1=crows[:, n].rearrange("p r c -> p c r"),
-                            op0=MULT,
-                            op1=ADD,
-                        )
+                    for i in range(per_bank):
+                        x = bank[:, 8 * columns * i : 8 * columns * (i + 1)].rearrange("p (c e) -> p c e", e=8)
+                        jobs += [(4 * (start + i) + j, x[:, :, 2 * j : 2 * j + 2]) for j in range(4)]
+                    base = 4 * per_bank * sub
+                    rotate_pairs(t, columns, jobs, lambda n: grid[:, (base + n) % 2, (base + n) // 2])
+                span = slice(8 * first, 8 * first + 16 * per_bank)
                 nc.gpsimd.tensor_scalar(
-                    out=out_tile[:, first : first + columns, slot, width * duo : width * duo + width].rearrange(
-                        "p c (j i r) -> p j c i r", i=2, r=2
-                    ),
-                    in0=rows.rearrange("p i j c r -> p j c i r"),
+                    out=result[:, :, span].rearrange("p c (m i r) -> p m c i r", i=2, r=2),
+                    in0=grid.rearrange("p i m c r -> p m c i r"),
                     scalar1=1.0,
                     scalar2=0.0,
                     op0=MULT,
                     op1=ADD,
                 )
+                if len(x_codes) < TILES and 2 * (first + 2 * per_bank) == BLOCKS:
+                    order_x_codes(len(x_codes))
 
-        def store(out_tile, batch, t0, slots):
-            heads = out_tile[:, HQ * batch : HQ * batch + HQ, slots].rearrange("p (h s) t d -> p s h t d", s=2)
-            first, last = t0 + slots.start, t0 + slots.stop
-            for s, dst in enumerate((q_rot, k_rot)):
+        def wide_products(t, batch, quarter):
+            bank = psum.tile([P, BANK], F32, name="bank")
+            span = slice(BANK * quarter, BANK * quarter + BANK)
+            multiply(bank[:], t, batch, w_raw[:, :, 2 * span.start : 2 * span.stop], w_plane[:, :, span])
+            x = bank[:].rearrange("p (c j r) -> p c j r", j=PAIRS, r=2)
+            with_cos = work.tile([P, 8, PAIRS, 2], F32, name="with_cos")
+            with_sin = work.tile([P, 2, 8, PAIRS], F32, name="with_sin")
+            at = slice(PAIRS * t, PAIRS * t + PAIRS)
+            for r, table in enumerate((neg_tab, sin_tab)):
+                nc.vector.tensor_tensor(
+                    out=with_sin[:, r],
+                    in0=x[:, :, :, 1 - r],
+                    in1=table[:, at].unsqueeze(1).to_broadcast([P, 8, PAIRS]),
+                    op=MULT,
+                )
+            nc.vector.tensor_tensor(
+                out=with_cos[:],
+                in0=x,
+                in1=cos_tab[:, at].unsqueeze(1).unsqueeze(3).to_broadcast([P, 8, PAIRS, 2]),
+                op=MULT,
+            )
+            return with_cos[:], with_sin[:].rearrange("p r c j -> p c j r")
+
+        def store(result, batch, head, t):
+            rows = result.rearrange("p (h s) t d -> p s h (t d)", s=2)
+            first = 16 * batch + head
+            for s, out in enumerate((q_rot, k_rot)):
                 nc.sync.dma_start(
-                    out=dst[16 * batch : 16 * batch + 16]
-                    .rearrange("h (p t) d -> p h t d", t=RUN)[:, :, first:last]
+                    out=out[first : first + result.shape[1] // 2]
+                    .rearrange("h (p t) d -> p h t d", t=TILES)[:, :, t : t + 2]
                     .rearrange("p h t d -> p h (t d)"),
-                    in_=heads[:, s].rearrange("p h t d -> p h (t d)"),
+                    in_=rows[:, s],
                 )
 
-        for t0 in range(0, RUN, 2):
-            out_tile = outs.tile([P, COLUMNS, 2, 64], F32, name="out_tile")
-            for batches in ((0, 1),) if t0 < 8 else ((0,), (1,)):
-                for slot in range(2):
-                    run_tile(t0 + slot, batches, out_tile, slot)
-                for batch in batches:
-                    store(out_tile, batch, t0, slice(0, 2))
+        for t in range(0, TILES - 2, 2):
+            pair = outs.tile([P, BATCH * HS, 2, DIM], F32, name="pair")
+            for i in range(2):
+                narrow(t + i, (0, 1), pair[:, :, i])
+            for batch in range(BATCH):
+                store(pair[:, HS * batch : HS * batch + HS], batch, 0, t)
+
+        t = TILES - 2
+        rest = outs.tile([P, HS, 2, DIM], F32, name="pair")
+        for i in range(2):
+            narrow(t + i, (0,), rest[:, :, i])
+        store(rest, 0, 0, t)
+        for quarter in range(4):
+            heads = work.tile([P, 8, 2, DIM], F32, name="heads")
+            adder = nc.vector if quarter == 3 else nc.gpsimd
+            products = [wide_products(t + i, 1, quarter) for i in range(2)]
+            for i, (with_cos, with_sin) in enumerate(products):
+                adder.tensor_tensor(
+                    out=heads[:, :, i].rearrange("p c (j r) -> p c j r", r=2), in0=with_cos, in1=with_sin, op=ADD
+                )
+            store(heads, 1, 4 * quarter, t)

from contextlib import ExitStack

import concourse.mybir as mybir

F32 = mybir.dt.float32
BF16 = mybir.dt.bfloat16
I32 = mybir.dt.int32
U8 = mybir.dt.uint8
FP4 = mybir.dt.float4_e2m1fn_x4
ADD = mybir.AluOpType.add
MULT = mybir.AluOpType.mult
COPY = mybir.ActivationFunctionType.Copy

P = 128
GROUPS = 2
TOKENS = 2048
OUTS = 2048
BATCH = 2
TILES = 8
PAIRS = 32
DIM = 2 * PAIRS
HS = 32
BLOCKS = 8
BLOCK = 256
BANK = 512
FLOPS = 2 * TOKENS * OUTS * 1024


def tile_repro_pa_kernel(tc, x_words, x_scales, w_words, w_scales, cos, sin, q_rot, k_rot):
    nc = tc.nc
    with ExitStack() as ctx:
        keep = ctx.enter_context(tc.tile_pool(name="keep", bufs=1))
        work = ctx.enter_context(tc.tile_pool(name="work", bufs=4))
        sines = ctx.enter_context(tc.tile_pool(name="sines", bufs=6))
        outs = ctx.enter_context(tc.tile_pool(name="outs", bufs=3))
        psum = ctx.enter_context(tc.psum_pool(name="psum", bufs=8))
        ctx.enter_context(tc.manual_schedule())

        x_plane = keep.tile([P, GROUPS, TOKENS], U8, align_bytes=64, name="x_plane")
        w_plane = keep.tile([P, GROUPS, OUTS], U8, align_bytes=64, name="w_plane")
        x_raw = keep.tile([P, GROUPS, 2 * TOKENS], U8, align_bytes=64, name="x_raw")
        w_raw = keep.tile([P, GROUPS, 2 * OUTS], U8, align_bytes=64, name="w_raw")
        cos_in = keep.tile([P, TILES * PAIRS], BF16, name="cos_in")
        sin_in = keep.tile([P, TILES * PAIRS], BF16, name="sin_in")
        cos_tab = keep.tile([P, TILES * PAIRS], F32, name="cos_tab")
        sin_tab = keep.tile([P, TILES * PAIRS], F32, name="sin_tab")
        neg_tab = keep.tile([P, TILES * PAIRS], F32, name="neg_tab")

        def load_codes(tile, words):
            nc.sync.dma_start(out=tile[:].bitcast(I32), in_=words.rearrange("g p n -> p g n").bitcast(I32))

        def load_scales(plane, scales):
            for quad in range(4):
                nc.sync.dma_start(
                    out=plane[32 * quad : 32 * quad + 4].bitcast(I32),
                    in_=scales[:, 4 * quad : 4 * quad + 4].rearrange("g r n -> r g n").bitcast(I32),
                )

        nc.vector.memset(x_plane[:].rearrange("p g n -> p (g n)").bitcast(I32), 0)
        nc.vector.memset(w_plane[:].rearrange("p g n -> p (g n)").bitcast(I32), 0)
        load_scales(x_plane, x_scales)
        load_codes(x_raw, x_words)
        load_codes(w_raw, w_words)
        load_scales(w_plane, w_scales)
        nc.gpsimd.dma_start(out=sin_in[:], in_=sin.rearrange("(p t) j -> p (t j)", t=TILES))
        nc.gpsimd.dma_start(out=cos_in[:], in_=cos.rearrange("(p t) j -> p (t j)", t=TILES))
        nc.scalar.activation(out=sin_tab[:], in_=sin_in[:], func=COPY)
        nc.scalar.activation(out=neg_tab[:], in_=sin_in[:], func=COPY, scale=-1.0)
        nc.scalar.activation(out=cos_tab[:], in_=cos_in[:], func=COPY)

        x_codes, x_bytes, w_codes, w_bytes = [], [], [], []

        def order_x_bytes(t):
            tile = keep.tile([P, GROUPS, BATCH, P], U8, align_bytes=64, name=f"x_bytes{t}")
            nc.vector.tensor_copy(
                out=tile[:], in_=x_plane[:].rearrange("p g (q t b) -> p t g b q", t=TILES, b=BATCH)[:, t]
            )
            x_bytes.append(tile)

        def order_x_codes(t):
            tile = keep.tile([P, GROUPS, BATCH, P, 2], U8, align_bytes=64, name=f"x_codes{t}")
            nc.vector.tensor_copy(
                out=tile[:], in_=x_raw[:].rearrange("p g (q t b c) -> p t g b q c", t=TILES, b=BATCH, c=2)[:, t]
            )
            x_codes.append(tile)

        def order_w(source, width, name, block):
            words = 8 * width // 4
            tile = keep.tile([P, GROUPS, BLOCK * width], U8, align_bytes=64, name=f"{name}{block}")
            nc.vector.tensor_copy(
                out=tile[:].bitcast(I32).rearrange("p g (h w) -> p g h w", w=words),
                in_=source[:].bitcast(I32).rearrange("p g (h i w) -> p i g h w", i=BLOCKS, w=words)[:, block],
            )
            return tile

        for t in range(TILES):
            order_x_bytes(t)
        order_x_codes(0)
        for block in range(BLOCKS):
            w_codes.append(order_w(w_raw, 2, "w_codes", block))
            w_bytes.append(order_w(w_plane, 1, "w_bytes", block))

        def multiply(out, t, batch, codes, scales):
            for g in range(GROUPS):
                nc.tensor.matmul_mx(
                    out=out,
                    lhsT=x_codes[t][:, g, batch].rearrange("p q c -> p (q c)").bitcast(FP4),
                    lhsT_scale=x_bytes[t][:, g, batch],
                    rhs=codes[:, g].bitcast(FP4),
                    rhs_scale=scales[:, g],
                    start=(g == 0),
                    stop=(g == GROUPS - 1),
                )

        def rotate_pairs(t, columns, jobs, turned):
            product = sines.tile([P, BANK], F32, name="product")
            rows = product[:].rearrange("p (n r c) -> p n r c", r=2, c=columns)
            for n, (k, x) in enumerate(jobs):
                at = slice(PAIRS * t + k, PAIRS * t + k + 1)
                nc.scalar.activation(out=rows[:, n, 0], in_=x[:, :, 1], func=COPY, scale=neg_tab[:, at])
                nc.scalar.activation(out=rows[:, n, 1], in_=x[:, :, 0], func=COPY, scale=sin_tab[:, at])
            for n, (k, x) in reversed(list(enumerate(jobs))):
                nc.vector.scalar_tensor_tensor(
                    out=turned(n),
                    in0=x,
                    scalar=cos_tab[:, PAIRS * t + k : PAIRS * t + k + 1],
                    in1=rows[:, n].rearrange("p r c -> p c r"),
                    op0=MULT,
                    op1=ADD,
                )

        def narrow(t, batches, result):
            columns = HS * len(batches)
            per_bank = 2 // len(batches)
            for first in range(0, BLOCKS, 2 * per_bank):
                turned = work.tile([P, 2 * BANK], F32, name="turned")
                grid = turned[:].rearrange("p (i m c r) -> p i m c r", i=2, c=columns, r=2)
                for sub in range(2):
                    start = first + sub * per_bank
                    bank = psum.tile([P, BANK], F32, name="bank")
                    halves = [(b, start + i) for i in range(per_bank) for b in batches]
                    for half, (b, block) in enumerate(halves):
                        multiply(bank[:, BLOCK * half : BLOCK * half + BLOCK], t, b, w_codes[block], w_bytes[block])
                    jobs = []
                    for i in range(per_bank):
                        x = bank[:, 8 * columns * i : 8 * columns * (i + 1)].rearrange("p (c e) -> p c e", e=8)
                        jobs += [(4 * (start + i) + j, x[:, :, 2 * j : 2 * j + 2]) for j in range(4)]
                    base = 4 * per_bank * sub
                    rotate_pairs(t, columns, jobs, lambda n: grid[:, (base + n) % 2, (base + n) // 2])
                span = slice(8 * first, 8 * first + 16 * per_bank)
                nc.gpsimd.tensor_scalar(
                    out=result[:, :, span].rearrange("p c (m i r) -> p m c i r", i=2, r=2),
                    in0=grid.rearrange("p i m c r -> p m c i r"),
                    scalar1=1.0,
                    scalar2=0.0,
                    op0=MULT,
                    op1=ADD,
                )
                if len(x_codes) < TILES and 2 * (first + 2 * per_bank) == BLOCKS:
                    order_x_codes(len(x_codes))

        def wide_products(t, batch, quarter):
            bank = psum.tile([P, BANK], F32, name="bank")
            span = slice(BANK * quarter, BANK * quarter + BANK)
            multiply(bank[:], t, batch, w_raw[:, :, 2 * span.start : 2 * span.stop], w_plane[:, :, span])
            x = bank[:].rearrange("p (c j r) -> p c j r", j=PAIRS, r=2)
            with_cos = work.tile([P, 8, PAIRS, 2], F32, name="with_cos")
            with_sin = work.tile([P, 2, 8, PAIRS], F32, name="with_sin")
            at = slice(PAIRS * t, PAIRS * t + PAIRS)
            for r, table in enumerate((neg_tab, sin_tab)):
                nc.vector.tensor_tensor(
                    out=with_sin[:, r],
                    in0=x[:, :, :, 1 - r],
                    in1=table[:, at].unsqueeze(1).to_broadcast([P, 8, PAIRS]),
                    op=MULT,
                )
            nc.vector.tensor_tensor(
                out=with_cos[:],
                in0=x,
                in1=cos_tab[:, at].unsqueeze(1).unsqueeze(3).to_broadcast([P, 8, PAIRS, 2]),
                op=MULT,
            )
            return with_cos[:], with_sin[:].rearrange("p r c j -> p c j r")

        def store(result, batch, head, t):
            rows = result.rearrange("p (h s) t d -> p s h (t d)", s=2)
            first = 16 * batch + head
            for s, out in enumerate((q_rot, k_rot)):
                nc.sync.dma_start(
                    out=out[first : first + result.shape[1] // 2]
                    .rearrange("h (p t) d -> p h t d", t=TILES)[:, :, t : t + 2]
                    .rearrange("p h t d -> p h (t d)"),
                    in_=rows[:, s],
                )

        for t in range(0, TILES - 2, 2):
            pair = outs.tile([P, BATCH * HS, 2, DIM], F32, name="pair")
            for i in range(2):
                narrow(t + i, (0, 1), pair[:, :, i])
            for batch in range(BATCH):
                store(pair[:, HS * batch : HS * batch + HS], batch, 0, t)

        t = TILES - 2
        rest = outs.tile([P, HS, 2, DIM], F32, name="pair")
        for i in range(2):
            narrow(t + i, (0,), rest[:, :, i])
        store(rest, 0, 0, t)
        for quarter in range(4):
            heads = work.tile([P, 8, 2, DIM], F32, name="heads")
            adder = nc.vector if quarter == 3 else nc.gpsimd
            products = [wide_products(t + i, 1, quarter) for i in range(2)]
            for i, (with_cos, with_sin) in enumerate(products):
                adder.tensor_tensor(
                    out=heads[:, :, i].rearrange("p c (j r) -> p c j r", r=2), in0=with_cos, in1=with_sin, op=ADD
                )
            store(heads, 1, 4 * quarter, t)
